import numpy as np
import ml_dtypes


def mxq(x, axis, fmt="e4m3"):
    dtype, down = {"e4m3": (ml_dtypes.float8_e4m3fn, 7), "e5m2": (ml_dtypes.float8_e5m2, 14)}[fmt]
    v = np.moveaxis(np.asarray(x, np.float32).astype(ml_dtypes.bfloat16).astype(np.float64), axis, -1)
    blocks = v.reshape(v.shape[:-1] + (-1, 32))
    amax = np.abs(blocks).max(-1, keepdims=True)
    byte = np.maximum(np.where(amax > 0, np.frexp(amax)[1] - 1 + 127, 0) - down, 1)
    scale = np.exp2(byte - 127.0)
    codes = (blocks / scale).astype(np.float32).astype(dtype).astype(np.float64)
    return np.moveaxis((codes * scale).reshape(v.shape), -1, axis)


WIDE = False


def mx_kscale(k):
    if not WIDE:
        return np.ones(k)
    levels = np.array([10, -10, 5, -5, 0])
    a = np.random.permutation(np.resize(levels, k // 512 * 4)).reshape(k // 512, 4)
    idx = np.arange(k)
    return np.exp2(a[idx // 512, idx % 128 // 32])


BF16 = ml_dtypes.bfloat16


def bf(x):
    return np.asarray(x, np.float32).astype(BF16)


def f64(x):
    return np.asarray(x).astype(np.float64)


E2M1 = np.array([0.0, 0.5, 1.0, 1.5, 2.0, 3.0, 4.0, 6.0, -0.0, -0.5, -1.0, -1.5, -2.0, -3.0, -4.0, -6.0])


def pack_weight(w, fmt):
    k, n = w.shape
    w = f64(bf(w)).reshape(k // 32, 32, n)
    amax = np.abs(w).max(1)
    if fmt == "e4m3":
        byte = np.frexp(amax)[1] - 1 + 127 - 7
    else:
        mant, ex = np.frexp(amax / 6.0)
        byte = np.where(mant > 0.5, ex, ex - 1) + 127
    byte = np.clip(np.where(amax > 0, byte, 1), 1, 254)
    scaled = (w * np.exp2(127.0 - byte)[:, None, :]).reshape(k, n).astype(np.float32)
    by_word = np.ascontiguousarray(scaled.reshape(k // 512, 128, 4, n).transpose(0, 1, 3, 2))
    if fmt == "e4m3":
        words = by_word.astype(ml_dtypes.float8_e4m3fn).view(np.uint8)
    else:
        c = by_word.astype(ml_dtypes.float4_e2m1fn).view(np.uint8) & 0xF
        words = c[..., 0::2] | (c[..., 1::2] << 4)
    return np.ascontiguousarray(words), np.ascontiguousarray(byte.astype(np.uint8).reshape(k // 512, 16, n))


def unpack_weight(words, scales, fmt):
    g, p, n, _ = words.shape
    if fmt == "e4m3":
        vals = np.ascontiguousarray(words).view(ml_dtypes.float8_e4m3fn).astype(np.float64)
    else:
        nib = np.empty((g, p, n, 4), np.uint8)
        nib[..., 0::2] = words & 0xF
        nib[..., 1::2] = words >> 4
        vals = E2M1[nib]
    vals = vals * np.repeat(np.exp2(scales.astype(np.float64) - 127.0), 8, axis=1)[..., None]
    return vals.transpose(0, 1, 3, 2).reshape(g * 512, n)

def pack4(w):
    words, scales = pack_weight(w, "e2m1")
    return words.reshape(words.shape[0], 128, -1), scales


def unpack4(words, scales):
    return unpack_weight(words.reshape(words.shape[0], 128, -1, 2), scales, "e2m1")


B, S, H, D = 2, 512, 16, 64
E = H * D
HALF = D // 2


def rotate_half(u):
    u1, u2 = np.split(u, 2, axis=-1)
    return np.concatenate([-u2, u1], axis=-1)


def apply_rope(t, sin, cos):
    x1, x2 = np.split(t, 2, axis=-1)
    x_rot = x1 * cos + rotate_half(x1) * sin
    return np.concatenate([x_rot, x2], axis=-1)


def setup_inputs():
    s = mx_kscale(E)
    th = np.random.uniform(0.0, 2.0 * np.pi, (S, HALF))
    x = bf(np.random.standard_normal((B, S, E)) * s)
    words, scales = pack4(np.random.standard_normal((E, 3 * E)) / np.sqrt(E) / s[:, None])
    return {"x": x,
            "W_qkv_words": words,
            "W_qkv_scales": scales,
            "b_qkv": bf(np.random.standard_normal(3 * E) * 0.2),
            "sin_tab": bf(np.sin(th)),
            "cos_tab": bf(np.cos(th))}


def reference(x, W_qkv_words, W_qkv_scales, b_qkv, sin_tab, cos_tab):
    qkv = (mxq(f64(x), 2, "e4m3") @ unpack4(W_qkv_words, W_qkv_scales)) + f64(b_qkv)
    q, k, v = np.split(qkv, 3, axis=-1)
    q = q.reshape(B, S, H, D)
    k = k.reshape(B, S, H, D)
    v = v.reshape(B, S, H, D)
    sin = f64(sin_tab)[None, :, None, :]
    cos = f64(cos_tab)[None, :, None, :]
    q_rot = apply_rope(q, sin, cos)
    k_rot = apply_rope(k, sin, cos)
    return q_rot, k_rot, v

@@ -1,0 +1,215 @@
+from contextlib import ExitStack
+
+import concourse.mybir as mybir
+from concourse.masks import make_identity
+
+F32 = mybir.dt.float32
+BF16 = mybir.dt.bfloat16
+I32 = mybir.dt.int32
+U8 = mybir.dt.uint8
+U32 = mybir.dt.uint32
+FP8X4 = mybir.dt.float8_e4m3fn_x4
+FP4X4 = mybir.dt.float4_e2m1fn_x4
+ADD = mybir.AluOpType.add
+MULT = mybir.AluOpType.mult
+
+P = 128
+TOKENS = 1024
+POSITIONS = 512
+K = 1024
+PASSES = K // (4 * P)
+HEADS = 16
+D = 64
+HALF = D // 2
+QUARTER = HALF // 2
+E = HEADS * D
+BANK = 512
+BANK_HEADS = BANK // D
+TOKEN_TILES = TOKENS // P
+POSITION_TILES = POSITIONS // P
+
+FLOPS = 2 * TOKENS * K * 3 * E
+
+
+def tile_improvedattention_pa_kernel(
+    tc, x, w_words, w_scales, b_qkv, sin_tab, cos_tab, out_q, out_k, out_v
+):
+    nc = tc.nc
+    x_rows = x.flatten_outer_dims()
+    out_rows = [o.rearrange("b s h d -> (b s) (h d)") for o in (out_q, out_k, out_v)]
+
+    with ExitStack() as ctx:
+        keep = ctx.enter_context(tc.tile_pool(name="keep", bufs=1))
+        stage = ctx.enter_context(tc.tile_pool(name="stage", bufs=2))
+        results = ctx.enter_context(tc.tile_pool(name="results", bufs=3))
+        psum_flip = ctx.enter_context(tc.psum_pool(name="psum_flip", bufs=2))
+        psum_acc = ctx.enter_context(tc.psum_pool(name="psum_acc", bufs=6))
+
+        w_planes = keep.tile([P, PASSES, 3 * E], U8, align_bytes=64)
+        nc.vector.memset(w_planes[:].bitcast(I32), 0)
+
+        x_all = keep.tile([P, TOKEN_TILES, K], BF16)
+        nc.sync.dma_start(out=x_all[:, 0, :], in_=x_rows[0:P, :])
+
+        scale_words = w_scales.bitcast(I32)
+        for low in range(2):
+            for r in range(4):
+                nc.sync.dma_start(
+                    out=w_planes[32 * low + r : P : 64, :, :].bitcast(I32),
+                    in_=scale_words[:, 4 * low + r : 16 : 8, :].rearrange("g c n -> c g n"),
+                )
+
+        w_codes = keep.tile([P, PASSES, 2 * 3 * E], U8, align_bytes=64)
+        for third in range(3):
+            cols = slice(2 * E * third, 2 * E * (third + 1))
+            nc.sync.dma_start(
+                out=w_codes[:, :, cols].bitcast(I32),
+                in_=w_words[:, :, cols].bitcast(I32).rearrange("g p c -> p g c"),
+            )
+            nc.sync.dma_start(out=x_all[:, third + 1, :], in_=x_rows[P * (third + 1) : P * (third + 2), :])
+        for t in range(4, TOKEN_TILES):
+            nc.sync.dma_start(out=x_all[:, t, :], in_=x_rows[P * t : P * (t + 1), :])
+
+        table = keep.tile([P, POSITION_TILES, P], BF16)
+        cos_view = cos_tab.rearrange("(t p) j -> p t j", p=P)
+        sin_view = sin_tab.rearrange("(t p) j -> p t j", p=P)
+        nc.scalar.dma_start(out=table[:, :, 0:HALF], in_=cos_view)
+        nc.scalar.dma_start(out=table[:, :, HALF : HALF + QUARTER], in_=sin_view[:, :, QUARTER:HALF])
+        nc.scalar.dma_start(out=table[:, :, HALF + QUARTER : D], in_=sin_view[:, :, 0:QUARTER])
+        nc.vector.memset(table[:, :, D:P], 0.0)
+        nc.vector.tensor_scalar_mul(
+            out=table[:, :, HALF + QUARTER : D], in0=table[:, :, HALF + QUARTER : D], scalar1=-1.0
+        )
+
+        bias = keep.tile([P, 3 * E], BF16)
+        nc.scalar.dma_start(out=bias[:], in_=b_qkv.partition_broadcast(P))
+
+        ident_f32 = keep.tile([P, P], F32)
+        make_identity(nc, ident_f32[:])
+        ident_bf16 = keep.tile([P, P], BF16)
+        make_identity(nc, ident_bf16[:])
+
+        x_codes = keep.tile([P, TOKEN_TILES, PASSES, P], U32, align_bytes=64)
+        x_planes = keep.tile([P, TOKEN_TILES, PASSES, P], U8, align_bytes=64)
+
+        def quantise_tokens(t):
+            words = x_all[:, t, :].bitcast(F32)
+            flipped = psum_flip.tile([P, PASSES, 2, P], F32, tag="flip")
+            for g in range(PASSES):
+                for u in range(2):
+                    nc.tensor.transpose(
+                        flipped[:, g, u, :], words[:, 256 * g + u : 256 * (g + 1) : 2], ident_f32[:]
+                    )
+            grouped = stage.tile([P, PASSES, P, 4], BF16, align_bytes=64)
+            nc.scalar.copy(out=grouped[:].bitcast(F32), in_=flipped[:].rearrange("p g u r -> p g r u"))
+            nc.vector.quantize_mx(
+                out=x_codes[:, t].rearrange("p g r -> p (g r)").bitcast(FP8X4),
+                scales=x_planes[:, t].rearrange("p g r -> p (g r)"),
+                in_=grouped[:].rearrange("p g r j -> p (g r j)"),
+            )
+
+        quantise_tokens(0)
+
+        bias_qk = bias[:, 0 : 2 * E].rearrange("p (q d) -> p q d", d=D)
+        diagonals = keep.tile([P, 2 * HEADS, HALF], BF16)
+        nc.gpsimd.memset(diagonals[D:P], 0.0)
+
+        def spread(rows, width, cols, features, ident_cols):
+            nc.vector.tensor_tensor(
+                out=diagonals[rows, :, cols],
+                in0=bias_qk[rows, :, features],
+                in1=ident_bf16[rows, ident_cols].unsqueeze(1).to_broadcast([HALF, 2 * HEADS, width]),
+                op=MULT,
+            )
+
+        spread(slice(0, HALF), HALF, slice(0, HALF), slice(0, HALF), slice(0, HALF))
+        spread(slice(HALF, D), QUARTER, slice(0, QUARTER), slice(QUARTER, HALF), slice(HALF + QUARTER, D))
+        spread(slice(HALF, D), QUARTER, slice(QUARTER, HALF), slice(0, QUARTER), slice(HALF, HALF + QUARTER))
+
+        table_flipped = psum_flip.tile([P, POSITION_TILES, P], BF16, tag="flip")
+        for pt in range(POSITION_TILES):
+            nc.tensor.transpose(table_flipped[:, pt, :], table[:, pt, :], ident_bf16[:])
+        table_t = keep.tile([P, POSITION_TILES, P], BF16)
+        nc.scalar.copy(out=table_t[:], in_=table_flipped[:])
+
+        turned_bias = keep.tile([P, POSITION_TILES, 2 * HEADS, HALF], F32)
+        diagonal_cols = diagonals[:].rearrange("p q j -> p (q j)")
+        for pt in range(POSITION_TILES):
+            for third in range(2):
+                made = psum_acc.tile([P, BANK], F32, tag="acc")
+                nc.tensor.matmul(
+                    out=made[:],
+                    lhsT=table_t[:, pt, :],
+                    rhs=diagonal_cols[:, BANK * third : BANK * (third + 1)],
+                    start=True,
+                    stop=True,
+                )
+                nc.scalar.copy(
+                    out=turned_bias[:, pt, HEADS * third : HEADS * (third + 1), :].rearrange("p q j -> p (q j)"),
+                    in_=made[:],
+                )
+
+        for t in range(TOKEN_TILES):
+            if t + 1 < TOKEN_TILES:
+                quantise_tokens(t + 1)
+            pt = t % POSITION_TILES
+            factors = table[:, pt, 0:D].rearrange("p (c j) -> p c j", c=2).unsqueeze(1)
+            for third in range(3):
+                turned = third < 2
+                result = results.tile([P, HEADS, D], F32)
+                if turned:
+                    products = results.tile([P, HEADS, 2, HALF], F32)
+                for block in range(E // BANK):
+                    n = (E // BANK) * third + block
+                    acc = psum_acc.tile([P, BANK], F32, tag="acc")
+                    for g in range(PASSES):
+                        nc.tensor.matmul_mx(
+                            out=acc[:],
+                            lhsT=x_codes[:, t, g, :].bitcast(FP8X4),
+                            lhsT_scale=x_planes[:, t, g, :],
+                            rhs=w_codes[:, g, 2 * BANK * n : 2 * BANK * (n + 1)].bitcast(FP4X4),
+                            rhs_scale=w_planes[:, g, BANK * n : BANK * (n + 1)],
+                            start=(g == 0),
+                            stop=(g == PASSES - 1),
+                        )
+                    heads = slice(BANK_HEADS * block, BANK_HEADS * (block + 1))
+                    acc_heads = acc[:].rearrange("p (h d) -> p h d", d=D)
+                    bias_heads = bias[:, BANK * n : BANK * (n + 1)].rearrange("p (h d) -> p h d", d=D)
+                    if not turned:
+                        nc.vector.tensor_tensor(out=result[:, heads, :], in0=acc_heads, in1=bias_heads, op=ADD)
+                    else:
+                        nc.vector.tensor_tensor(
+                            out=result[:, heads, HALF:D],
+                            in0=acc_heads[:, :, HALF:D],
+                            in1=bias_heads[:, :, HALF:D],
+                            op=ADD,
+                        )
+                        nc.vector.tensor_tensor(
+                            out=products[:, heads, :, :],
+                            in0=acc_heads[:, :, 0:HALF].unsqueeze(2).to_broadcast([P, BANK_HEADS, 2, HALF]),
+                            in1=factors.to_broadcast([P, BANK_HEADS, 2, HALF]),
+                            op=MULT,
+                        )
+                if turned:
+                    nc.gpsimd.tensor_tensor(
+                        out=products[:, :, 0, :],
+                        in0=products[:, :, 0, :],
+                        in1=turned_bias[:, pt, HEADS * third : HEADS * (third + 1), :],
+                        op=ADD,
+                    )
+                    nc.gpsimd.tensor_tensor(
+                        out=result[:, :, 0:QUARTER],
+                        in0=products[:, :, 0, 0:QUARTER],
+                        in1=products[:, :, 1, QUARTER:HALF],
+                        op=ADD,
+                    )
+                    nc.gpsimd.tensor_tensor(
+                        out=result[:, :, QUARTER:HALF],
+                        in0=products[:, :, 0, QUARTER:HALF],
+                        in1=products[:, :, 1, 0:QUARTER],
+                        op=ADD,
+                    )
+                nc.sync.dma_start(
+                    out=out_rows[third][P * t : P * (t + 1), :],
+                    in_=result[:].rearrange("p h d -> p (h d)"),
+                )

@@ -14,7 +14,7 @@ ADD = mybir.AluOpType.add
 MULT = mybir.AluOpType.mult
 
 P = 128
-TOKENS = 1024
+BATCH = 2
 POSITIONS = 512
 K = 1024
 PASSES = K // (4 * P)
@@ -25,10 +25,12 @@ QUARTER = HALF // 2
 E = HEADS * D
 BANK = 512
 BANK_HEADS = BANK // D
-TOKEN_TILES = TOKENS // P
+BANKS = 3 * E // BANK
+TURNED_BANKS = 2 * E // BANK
 POSITION_TILES = POSITIONS // P
+TOKEN_TILES = BATCH * POSITION_TILES
 
-FLOPS = 2 * TOKENS * K * 3 * E
+FLOPS = 2 * BATCH * POSITIONS * K * 3 * E
 
 
 def tile_improvedattention_pa_kernel(
@@ -41,53 +43,56 @@ def tile_improvedattention_pa_kernel(
     with ExitStack() as ctx:
         keep = ctx.enter_context(tc.tile_pool(name="keep", bufs=1))
         stage = ctx.enter_context(tc.tile_pool(name="stage", bufs=2))
-        results = ctx.enter_context(tc.tile_pool(name="results", bufs=3))
+        results = ctx.enter_context(tc.tile_pool(name="results", bufs=4))
+        partial = ctx.enter_context(tc.tile_pool(name="partial", bufs=3))
         psum_flip = ctx.enter_context(tc.psum_pool(name="psum_flip", bufs=2))
-        psum_acc = ctx.enter_context(tc.psum_pool(name="psum_acc", bufs=6))
+        psum_acc = ctx.enter_context(tc.psum_pool(name="psum_acc", bufs=BANKS))
 
         w_planes = keep.tile([P, PASSES, 3 * E], U8, align_bytes=64)
         nc.vector.memset(w_planes[:].bitcast(I32), 0)
+        scale_words = w_scales.bitcast(I32)
+        for r in range(4):
+            nc.sync.dma_start(
+                out=w_planes[r:P:32, :, :].bitcast(I32),
+                in_=scale_words[:, r:16:4, :].rearrange("g c n -> c g n"),
+            )
 
         x_all = keep.tile([P, TOKEN_TILES, K], BF16)
-        nc.sync.dma_start(out=x_all[:, 0, :], in_=x_rows[0:P, :])
-
-        scale_words = w_scales.bitcast(I32)
-        for low in range(2):
-            for r in range(4):
-                nc.sync.dma_start(
-                    out=w_planes[32 * low + r : P : 64, :, :].bitcast(I32),
-                    in_=scale_words[:, 4 * low + r : 16 : 8, :].rearrange("g c n -> c g n"),
-                )
-
         w_codes = keep.tile([P, PASSES, 2 * 3 * E], U8, align_bytes=64)
-        for third in range(3):
+        sin_raw = keep.tile([P, POSITION_TILES, HALF], BF16)
+        table = keep.tile([P, POSITION_TILES, P], BF16)
+        bias = keep.tile([P, 3 * E], BF16)
+
+        def load_x(t):
+            nc.sync.dma_start(out=x_all[:, t, :], in_=x_rows[P * t : P * (t + 1), :])
+
+        def load_w(third):
             cols = slice(2 * E * third, 2 * E * (third + 1))
             nc.sync.dma_start(
                 out=w_codes[:, :, cols].bitcast(I32),
                 in_=w_words[:, :, cols].bitcast(I32).rearrange("g p c -> p g c"),
             )
-            nc.sync.dma_start(out=x_all[:, third + 1, :], in_=x_rows[P * (third + 1) : P * (third + 2), :])
-        for t in range(4, TOKEN_TILES):
-            nc.sync.dma_start(out=x_all[:, t, :], in_=x_rows[P * t : P * (t + 1), :])
 
-        table = keep.tile([P, POSITION_TILES, P], BF16)
-        cos_view = cos_tab.rearrange("(t p) j -> p t j", p=P)
-        sin_view = sin_tab.rearrange("(t p) j -> p t j", p=P)
-        nc.scalar.dma_start(out=table[:, :, 0:HALF], in_=cos_view)
-        nc.scalar.dma_start(out=table[:, :, HALF : HALF + QUARTER], in_=sin_view[:, :, QUARTER:HALF])
-        nc.scalar.dma_start(out=table[:, :, HALF + QUARTER : D], in_=sin_view[:, :, 0:QUARTER])
-        nc.vector.memset(table[:, :, D:P], 0.0)
-        nc.vector.tensor_scalar_mul(
-            out=table[:, :, HALF + QUARTER : D], in0=table[:, :, HALF + QUARTER : D], scalar1=-1.0
-        )
-
-        bias = keep.tile([P, 3 * E], BF16)
-        nc.scalar.dma_start(out=bias[:], in_=b_qkv.partition_broadcast(P))
+        load_x(0)
+        load_w(0)
+        nc.sync.dma_start(out=table[:, :, 0:HALF], in_=cos_tab.rearrange("(t p) j -> p t j", p=P))
+        nc.sync.dma_start(out=sin_raw[:], in_=sin_tab.rearrange("(t p) j -> p t j", p=P))
+        nc.sync.dma_start(out=bias[:], in_=b_qkv.partition_broadcast(P))
+        load_x(1)
+        load_w(1)
+        load_x(2)
+        load_w(2)
+        for t in range(3, TOKEN_TILES):
+            load_x(t)
 
         ident_f32 = keep.tile([P, P], F32)
         make_identity(nc, ident_f32[:])
         ident_bf16 = keep.tile([P, P], BF16)
         make_identity(nc, ident_bf16[:])
+
+        nc.scalar.copy(out=table[:, :, HALF : HALF + QUARTER], in_=sin_raw[:, :, QUARTER:HALF])
+        nc.scalar.mul(out=table[:, :, HALF + QUARTER : D], in_=sin_raw[:, :, 0:QUARTER], mul=-1.0)
+        nc.gpsimd.memset(table[:, :, D:P], 0.0)
 
         x_codes = keep.tile([P, TOKEN_TILES, PASSES, P], U32, align_bytes=64)
         x_planes = keep.tile([P, TOKEN_TILES, PASSES, P], U8, align_bytes=64)
@@ -113,103 +118,94 @@ def tile_improvedattention_pa_kernel(
         bias_qk = bias[:, 0 : 2 * E].rearrange("p (q d) -> p q d", d=D)
         diagonals = keep.tile([P, 2 * HEADS, HALF], BF16)
         nc.gpsimd.memset(diagonals[D:P], 0.0)
-
-        def spread(rows, width, cols, features, ident_cols):
-            nc.vector.tensor_tensor(
-                out=diagonals[rows, :, cols],
-                in0=bias_qk[rows, :, features],
-                in1=ident_bf16[rows, ident_cols].unsqueeze(1).to_broadcast([HALF, 2 * HEADS, width]),
-                op=MULT,
-            )
-
-        spread(slice(0, HALF), HALF, slice(0, HALF), slice(0, HALF), slice(0, HALF))
-        spread(slice(HALF, D), QUARTER, slice(0, QUARTER), slice(QUARTER, HALF), slice(HALF + QUARTER, D))
-        spread(slice(HALF, D), QUARTER, slice(QUARTER, HALF), slice(0, QUARTER), slice(HALF, HALF + QUARTER))
-
+        nc.vector.tensor_tensor(
+            out=diagonals[0:HALF],
+            in0=bias_qk[0:HALF, :, 0:HALF],
+            in1=ident_bf16[0:HALF, 0:HALF].unsqueeze(1).to_broadcast([HALF, 2 * HEADS, HALF]),
+            op=MULT,
+        )
+        nc.vector.tensor_tensor(
+            out=diagonals[HALF:D].rearrange("p q (f i) -> p q f i", f=2),
+            in0=bias_qk[HALF:D, :, 0:HALF].rearrange("p q (f i) -> p q f i", f=2)[:, :, ::-1, :],
+            in1=ident_bf16[HALF:D, HALF:D]
+            .rearrange("p (f i) -> p f i", f=2)[:, ::-1, :]
+            .unsqueeze(1)
+            .to_broadcast([HALF, 2 * HEADS, 2, QUARTER]),
+            op=MULT,
+        )
         table_flipped = psum_flip.tile([P, POSITION_TILES, P], BF16, tag="flip")
         for pt in range(POSITION_TILES):
             nc.tensor.transpose(table_flipped[:, pt, :], table[:, pt, :], ident_bf16[:])
         table_t = keep.tile([P, POSITION_TILES, P], BF16)
         nc.scalar.copy(out=table_t[:], in_=table_flipped[:])
+        turned_bias = keep.tile([P, POSITION_TILES, 2 * HEADS * HALF], F32)
 
-        turned_bias = keep.tile([P, POSITION_TILES, 2 * HEADS, HALF], F32)
-        diagonal_cols = diagonals[:].rearrange("p q j -> p (q j)")
-        for pt in range(POSITION_TILES):
-            for third in range(2):
+        def turn_bias(pt):
+            for half in range(2 * HEADS * HALF // BANK):
+                cols = slice(BANK * half, BANK * (half + 1))
                 made = psum_acc.tile([P, BANK], F32, tag="acc")
                 nc.tensor.matmul(
                     out=made[:],
                     lhsT=table_t[:, pt, :],
-                    rhs=diagonal_cols[:, BANK * third : BANK * (third + 1)],
+                    rhs=diagonals[:].rearrange("p q j -> p (q j)")[:, cols],
                     start=True,
                     stop=True,
                 )
-                nc.scalar.copy(
-                    out=turned_bias[:, pt, HEADS * third : HEADS * (third + 1), :].rearrange("p q j -> p (q j)"),
-                    in_=made[:],
-                )
+                nc.scalar.copy(out=turned_bias[:, pt, cols], in_=made[:])
 
         for t in range(TOKEN_TILES):
             if t + 1 < TOKEN_TILES:
                 quantise_tokens(t + 1)
             pt = t % POSITION_TILES
+            if t < POSITION_TILES:
+                turn_bias(pt)
+            sums = []
+            for n in range(BANKS):
+                acc = psum_acc.tile([P, BANK], F32, tag="acc")
+                for g in range(PASSES):
+                    nc.tensor.matmul_mx(
+                        out=acc[:],
+                        lhsT=x_codes[:, t, g, :].bitcast(FP8X4),
+                        lhsT_scale=x_planes[:, t, g, :],
+                        rhs=w_codes[:, g, 2 * BANK * n : 2 * BANK * (n + 1)].bitcast(FP4X4),
+                        rhs_scale=w_planes[:, g, BANK * n : BANK * (n + 1)],
+                        start=(g == 0),
+                        stop=(g == PASSES - 1),
+                    )
+                sums.append(acc[:].rearrange("p (h d) -> p h d", d=D))
+
             factors = table[:, pt, 0:D].rearrange("p (c j) -> p c j", c=2).unsqueeze(1)
+            products = partial.tile([P, 2 * HEADS, 2, HALF], F32)
+            for n in range(TURNED_BANKS):
+                nc.vector.tensor_tensor(
+                    out=products[:, BANK_HEADS * n : BANK_HEADS * (n + 1), :, :],
+                    in0=sums[n][:, :, 0:HALF].unsqueeze(2).to_broadcast([P, BANK_HEADS, 2, HALF]),
+                    in1=factors.to_broadcast([P, BANK_HEADS, 2, HALF]),
+                    op=MULT,
+                )
+            result = results.tile([P, 3 * HEADS, D], F32)
+            bias_heads = bias[:].rearrange("p (h d) -> p h d", d=D)
+            for n in range(BANKS):
+                heads = slice(BANK_HEADS * n, BANK_HEADS * (n + 1))
+                plain = slice(HALF, D) if n < TURNED_BANKS else slice(0, D)
+                nc.vector.tensor_tensor(
+                    out=result[:, heads, plain], in0=sums[n][:, :, plain], in1=bias_heads[:, heads, plain], op=ADD
+                )
+            turned = result[:, 0 : 2 * HEADS, 0:HALF]
+            nc.gpsimd.tensor_tensor(
+                out=turned.rearrange("p q (f i) -> p q f i", f=2),
+                in0=products[:, :, 0, :].rearrange("p q (f i) -> p q f i", f=2),
+                in1=products[:, :, 1, :].rearrange("p q (f i) -> p q f i", f=2)[:, :, ::-1, :],
+                op=ADD,
+            )
+            nc.gpsimd.tensor_tensor(
+                out=turned,
+                in0=turned,
+                in1=turned_bias[:, pt, :].rearrange("p (q j) -> p q j", j=HALF),
+                op=ADD,
+            )
             for third in range(3):
-                turned = third < 2
-                result = results.tile([P, HEADS, D], F32)
-                if turned:
-                    products = results.tile([P, HEADS, 2, HALF], F32)
-                for block in range(E // BANK):
-                    n = (E // BANK) * third + block
-                    acc = psum_acc.tile([P, BANK], F32, tag="acc")
-                    for g in range(PASSES):
-                        nc.tensor.matmul_mx(
-                            out=acc[:],
-                            lhsT=x_codes[:, t, g, :].bitcast(FP8X4),
-                            lhsT_scale=x_planes[:, t, g, :],
-                            rhs=w_codes[:, g, 2 * BANK * n : 2 * BANK * (n + 1)].bitcast(FP4X4),
-                            rhs_scale=w_planes[:, g, BANK * n : BANK * (n + 1)],
-                            start=(g == 0),
-                            stop=(g == PASSES - 1),
-                        )
-                    heads = slice(BANK_HEADS * block, BANK_HEADS * (block + 1))
-                    acc_heads = acc[:].rearrange("p (h d) -> p h d", d=D)
-                    bias_heads = bias[:, BANK * n : BANK * (n + 1)].rearrange("p (h d) -> p h d", d=D)
-                    if not turned:
-                        nc.vector.tensor_tensor(out=result[:, heads, :], in0=acc_heads, in1=bias_heads, op=ADD)
-                    else:
-                        nc.vector.tensor_tensor(
-                            out=result[:, heads, HALF:D],
-                            in0=acc_heads[:, :, HALF:D],
-                            in1=bias_heads[:, :, HALF:D],
-                            op=ADD,
-                        )
-                        nc.vector.tensor_tensor(
-                            out=products[:, heads, :, :],
-                            in0=acc_heads[:, :, 0:HALF].unsqueeze(2).to_broadcast([P, BANK_HEADS, 2, HALF]),
-                            in1=factors.to_broadcast([P, BANK_HEADS, 2, HALF]),
-                            op=MULT,
-                        )
-                if turned:
-                    nc.gpsimd.tensor_tensor(
-                        out=products[:, :, 0, :],
-                        in0=products[:, :, 0, :],
-                        in1=turned_bias[:, pt, HEADS * third : HEADS * (third + 1), :],
-                        op=ADD,
-                    )
-                    nc.gpsimd.tensor_tensor(
-                        out=result[:, :, 0:QUARTER],
-                        in0=products[:, :, 0, 0:QUARTER],
-                        in1=products[:, :, 1, QUARTER:HALF],
-                        op=ADD,
-                    )
-                    nc.gpsimd.tensor_tensor(
-                        out=result[:, :, QUARTER:HALF],
-                        in0=products[:, :, 0, QUARTER:HALF],
-                        in1=products[:, :, 1, 0:QUARTER],
-                        op=ADD,
-                    )
                 nc.sync.dma_start(
                     out=out_rows[third][P * t : P * (t + 1), :],
-                    in_=result[:].rearrange("p h d -> p (h d)"),
+                    in_=result[:, HEADS * third : HEADS * (third + 1), :].rearrange("p h d -> p (h d)"),
                 )

@@ -191,14 +191,15 @@ def tile_improvedattention_pa_kernel(
                 nc.vector.tensor_tensor(
                     out=result[:, heads, plain], in0=sums[n][:, :, plain], in1=bias_heads[:, heads, plain], op=ADD
                 )
+            adder = nc.vector if t == TOKEN_TILES - 1 else nc.gpsimd
             turned = result[:, 0 : 2 * HEADS, 0:HALF]
-            nc.gpsimd.tensor_tensor(
+            adder.tensor_tensor(
                 out=turned.rearrange("p q (f i) -> p q f i", f=2),
                 in0=products[:, :, 0, :].rearrange("p q (f i) -> p q f i", f=2),
                 in1=products[:, :, 1, :].rearrange("p q (f i) -> p q f i", f=2)[:, :, ::-1, :],
                 op=ADD,
             )
-            nc.gpsimd.tensor_tensor(
+            adder.tensor_tensor(
                 out=turned,
                 in0=turned,
                 in1=turned_bias[:, pt, :].rearrange("p (q j) -> p q j", j=HALF),

@@ -51,14 +51,11 @@ def tile_improvedattention_pa_kernel(
         w_planes = keep.tile([P, PASSES, 3 * E], U8, align_bytes=64)
         nc.vector.memset(w_planes[:].bitcast(I32), 0)
         scale_words = w_scales.bitcast(I32)
-        for r in range(4):
-            nc.sync.dma_start(
-                out=w_planes[r:P:32, :, :].bitcast(I32),
-                in_=scale_words[:, r:16:4, :].rearrange("g c n -> c g n"),
-            )
 
         x_all = keep.tile([P, TOKEN_TILES, K], BF16)
-        w_codes = keep.tile([P, PASSES, 2 * 3 * E], U8, align_bytes=64)
+        w_codes = [
+            keep.tile([P, PASSES, 2 * E], U8, align_bytes=64, name="w_codes_%d" % third) for third in range(3)
+        ]
         sin_raw = keep.tile([P, POSITION_TILES, HALF], BF16)
         table = keep.tile([P, POSITION_TILES, P], BF16)
         bias = keep.tile([P, 3 * E], BF16)
@@ -69,20 +66,28 @@ def tile_improvedattention_pa_kernel(
         def load_w(third):
             cols = slice(2 * E * third, 2 * E * (third + 1))
             nc.sync.dma_start(
-                out=w_codes[:, :, cols].bitcast(I32),
+                out=w_codes[third][:].bitcast(I32),
                 in_=w_words[:, :, cols].bitcast(I32).rearrange("g p c -> p g c"),
             )
 
+        b_rows = keep.tile([P, 2, 2, HALF], BF16)
+        nc.gpsimd.memset(b_rows[:], 0.0)
+        b_turned = b_qkv[0 : 2 * E].rearrange("(k e d) -> k e d", e=2, d=D)[:, :, 0:HALF]
         load_x(0)
         load_w(0)
+        load_w(1)
+        for r in range(4):
+            nc.sync.dma_start(
+                out=w_planes[r:P:32, :, :].bitcast(I32),
+                in_=scale_words[:, r:16:4, :].rearrange("g c n -> c g n"),
+            )
         nc.sync.dma_start(out=table[:, :, 0:HALF], in_=cos_tab.rearrange("(t p) j -> p t j", p=P))
         nc.sync.dma_start(out=sin_raw[:], in_=sin_tab.rearrange("(t p) j -> p t j", p=P))
-        nc.sync.dma_start(out=bias[:], in_=b_qkv.partition_broadcast(P))
+        nc.sync.dma_start(out=b_rows[0:HEADS, :, 0, :], in_=b_turned)
         load_x(1)
-        load_w(1)
-        load_x(2)
+        nc.sync.dma_start(out=bias[:], in_=b_qkv.partition_broadcast(P))
         load_w(2)
-        for t in range(3, TOKEN_TILES):
+        for t in range(2, TOKEN_TILES):
             load_x(t)
 
         ident_f32 = keep.tile([P, P], F32)
@@ -92,7 +97,7 @@ def tile_improvedattention_pa_kernel(
 
         nc.scalar.copy(out=table[:, :, HALF : HALF + QUARTER], in_=sin_raw[:, :, QUARTER:HALF])
         nc.scalar.mul(out=table[:, :, HALF + QUARTER : D], in_=sin_raw[:, :, 0:QUARTER], mul=-1.0)
-        nc.gpsimd.memset(table[:, :, D:P], 0.0)
+        nc.scalar.copy(out=table[:, :, D:P], in_=table[:, :, 0:D])
 
         x_codes = keep.tile([P, TOKEN_TILES, PASSES, P], U32, align_bytes=64)
         x_planes = keep.tile([P, TOKEN_TILES, PASSES, P], U8, align_bytes=64)
@@ -115,22 +120,19 @@ def tile_improvedattention_pa_kernel(
 
         quantise_tokens(0)
 
-        bias_qk = bias[:, 0 : 2 * E].rearrange("p (q d) -> p q d", d=D)
-        diagonals = keep.tile([P, 2 * HEADS, HALF], BF16)
-        nc.gpsimd.memset(diagonals[D:P], 0.0)
+        nc.scalar.copy(out=b_rows[:, :, 1, :], in_=b_rows[:, :, 0, :])
+        b_flipped = psum_flip.tile([P, P], BF16, tag="flip")
+        nc.tensor.transpose(b_flipped[:], b_rows[:].rearrange("p e c d -> p (e c d)"), ident_bf16[:])
+        b_cols = keep.tile([P, HEADS], BF16)
+        nc.scalar.copy(out=b_cols[:], in_=b_flipped[:, 0:HEADS])
+        ident_parts = ident_bf16[:].rearrange("p (e c f i) -> p e c f i", e=2, c=2, f=2)
+        place = keep.tile([P, 2, 2, QUARTER], BF16)
+        nc.vector.tensor_tensor(out=place[:], in0=ident_parts[:, :, 0, :, :], in1=ident_parts[:, :, 1, ::-1, :], op=ADD)
+        diagonals = keep.tile([P, HEADS, D], BF16)
         nc.vector.tensor_tensor(
-            out=diagonals[0:HALF],
-            in0=bias_qk[0:HALF, :, 0:HALF],
-            in1=ident_bf16[0:HALF, 0:HALF].unsqueeze(1).to_broadcast([HALF, 2 * HEADS, HALF]),
-            op=MULT,
-        )
-        nc.vector.tensor_tensor(
-            out=diagonals[HALF:D].rearrange("p q (f i) -> p q f i", f=2),
-            in0=bias_qk[HALF:D, :, 0:HALF].rearrange("p q (f i) -> p q f i", f=2)[:, :, ::-1, :],
-            in1=ident_bf16[HALF:D, HALF:D]
-            .rearrange("p (f i) -> p f i", f=2)[:, ::-1, :]
-            .unsqueeze(1)
-            .to_broadcast([HALF, 2 * HEADS, 2, QUARTER]),
+            out=diagonals[:],
+            in0=b_cols[:].unsqueeze(2).to_broadcast([P, HEADS, D]),
+            in1=place[:].rearrange("p e f i -> p (e f i)").unsqueeze(1).to_broadcast([P, HEADS, D]),
             op=MULT,
         )
         table_flipped = psum_flip.tile([P, POSITION_TILES, P], BF16, tag="flip")
@@ -143,7 +145,7 @@ def tile_improvedattention_pa_kernel(
         def turn_bias(pt):
             for half in range(2 * HEADS * HALF // BANK):
                 cols = slice(BANK * half, BANK * (half + 1))
-                made = psum_acc.tile([P, BANK], F32, tag="acc")
+                made = psum_flip.tile([P, BANK], F32, tag="flip")
                 nc.tensor.matmul(
                     out=made[:],
                     lhsT=table_t[:, pt, :],
@@ -154,20 +156,20 @@ def tile_improvedattention_pa_kernel(
                 nc.scalar.copy(out=turned_bias[:, pt, cols], in_=made[:])
 
         for t in range(TOKEN_TILES):
-            if t + 1 < TOKEN_TILES:
+            if 0 < t < TOKEN_TILES - 1:
                 quantise_tokens(t + 1)
             pt = t % POSITION_TILES
-            if t < POSITION_TILES:
-                turn_bias(pt)
             sums = []
             for n in range(BANKS):
+                if n == TURNED_BANKS and t < POSITION_TILES:
+                    turn_bias(pt)
                 acc = psum_acc.tile([P, BANK], F32, tag="acc")
                 for g in range(PASSES):
                     nc.tensor.matmul_mx(
                         out=acc[:],
                         lhsT=x_codes[:, t, g, :].bitcast(FP8X4),
                         lhsT_scale=x_planes[:, t, g, :],
-                        rhs=w_codes[:, g, 2 * BANK * n : 2 * BANK * (n + 1)].bitcast(FP4X4),
+                        rhs=w_codes[n // 2][:, g, 2 * BANK * (n % 2) : 2 * BANK * (n % 2 + 1)].bitcast(FP4X4),
                         rhs_scale=w_planes[:, g, BANK * n : BANK * (n + 1)],
                         start=(g == 0),
                         stop=(g == PASSES - 1),
@@ -183,6 +185,8 @@ def tile_improvedattention_pa_kernel(
                     in1=factors.to_broadcast([P, BANK_HEADS, 2, HALF]),
                     op=MULT,
                 )
+            if t == 0:
+                quantise_tokens(1)
             result = results.tile([P, 3 * HEADS, D], F32)
             bias_heads = bias[:].rearrange("p (h d) -> p h d", d=D)
             for n in range(BANKS):

@@ -48,6 +48,16 @@ def tile_improvedattention_pa_kernel(
         psum_flip = ctx.enter_context(tc.psum_pool(name="psum_flip", bufs=2))
         psum_acc = ctx.enter_context(tc.psum_pool(name="psum_acc", bufs=BANKS))
 
+        warm = keep.tile([P, BANK], BF16)
+        nc.vector.memset(warm[:], 0.0)
+
+        def warm_up(count):
+            for i in range(count):
+                idle = psum_acc.tile([P, BANK], F32, tag="acc")
+                nc.tensor.matmul(out=idle[:], lhsT=warm[:, 0:P], rhs=warm[:], start=True, stop=True)
+
+        warm_up(4)
+
         w_planes = keep.tile([P, PASSES, 3 * E], U8, align_bytes=64)
         nc.vector.memset(w_planes[:].bitcast(I32), 0)
         scale_words = w_scales.bitcast(I32)
@@ -73,6 +83,9 @@ def tile_improvedattention_pa_kernel(
         b_rows = keep.tile([P, 2, 2, HALF], BF16)
         nc.gpsimd.memset(b_rows[:], 0.0)
         b_turned = b_qkv[0 : 2 * E].rearrange("(k e d) -> k e d", e=2, d=D)[:, :, 0:HALF]
+        nc.sync.dma_start(out=b_rows[0:HEADS, :, 0, :], in_=b_turned)
+        nc.sync.dma_start(out=table[:, :, 0:HALF], in_=cos_tab.rearrange("(t p) j -> p t j", p=P))
+        nc.sync.dma_start(out=sin_raw[:], in_=sin_tab.rearrange("(t p) j -> p t j", p=P))
         load_x(0)
         load_w(0)
         load_w(1)
@@ -81,9 +94,6 @@ def tile_improvedattention_pa_kernel(
                 out=w_planes[r:P:32, :, :].bitcast(I32),
                 in_=scale_words[:, r:16:4, :].rearrange("g c n -> c g n"),
             )
-        nc.sync.dma_start(out=table[:, :, 0:HALF], in_=cos_tab.rearrange("(t p) j -> p t j", p=P))
-        nc.sync.dma_start(out=sin_raw[:], in_=sin_tab.rearrange("(t p) j -> p t j", p=P))
-        nc.sync.dma_start(out=b_rows[0:HEADS, :, 0, :], in_=b_turned)
         load_x(1)
         nc.sync.dma_start(out=bias[:], in_=b_qkv.partition_broadcast(P))
         load_w(2)
@@ -119,6 +129,7 @@ def tile_improvedattention_pa_kernel(
             )
 
         quantise_tokens(0)
+        warm_up(2)
 
         nc.scalar.copy(out=b_rows[:, :, 1, :], in_=b_rows[:, :, 0, :])
         b_flipped = psum_flip.tile([P, P], BF16, tag="flip")

@@ -57,6 +57,8 @@ def tile_improvedattention_pa_kernel(
                 nc.tensor.matmul(out=idle[:], lhsT=warm[:, 0:P], rhs=warm[:], start=True, stop=True)
 
         warm_up(4)
+        first = keep.tile([P, 1], BF16)
+        nc.scalar.copy(out=first[:], in_=warm[:, 0:1])
 
         w_planes = keep.tile([P, PASSES, 3 * E], U8, align_bytes=64)
         nc.vector.memset(w_planes[:].bitcast(I32), 0)
@@ -170,8 +172,12 @@ def tile_improvedattention_pa_kernel(
             if 0 < t < TOKEN_TILES - 1:
                 quantise_tokens(t + 1)
             pt = t % POSITION_TILES
-            sums = []
-            for n in range(BANKS):
+            last = t == TOKEN_TILES - 1
+            bank_order = list(range(BANKS))
+            if last:
+                bank_order = bank_order[TURNED_BANKS:] + bank_order[:TURNED_BANKS]
+            sums = {}
+            for n in bank_order:
                 if n == TURNED_BANKS and t < POSITION_TILES:
                     turn_bias(pt)
                 acc = psum_acc.tile([P, BANK], F32, tag="acc")
@@ -185,8 +191,28 @@ def tile_improvedattention_pa_kernel(
                         start=(g == 0),
                         stop=(g == PASSES - 1),
                     )
-                sums.append(acc[:].rearrange("p (h d) -> p h d", d=D))
+                sums[n] = acc[:].rearrange("p (h d) -> p h d", d=D)
 
+            result = results.tile([P, 3 * HEADS, D], F32)
+            bias_heads = bias[:].rearrange("p (h d) -> p h d", d=D)
+
+            def add_bias(n):
+                heads = slice(BANK_HEADS * n, BANK_HEADS * (n + 1))
+                plain = slice(HALF, D) if n < TURNED_BANKS else slice(0, D)
+                nc.vector.tensor_tensor(
+                    out=result[:, heads, plain], in0=sums[n][:, :, plain], in1=bias_heads[:, heads, plain], op=ADD
+                )
+
+            def store(third):
+                nc.sync.dma_start(
+                    out=out_rows[third][P * t : P * (t + 1), :],
+                    in_=result[:, HEADS * third : HEADS * (third + 1), :].rearrange("p h d -> p (h d)"),
+                )
+
+            if last:
+                for n in range(TURNED_BANKS, BANKS):
+                    add_bias(n)
+                store(2)
             factors = table[:, pt, 0:D].rearrange("p (c j) -> p c j", c=2).unsqueeze(1)
             products = partial.tile([P, 2 * HEADS, 2, HALF], F32)
             for n in range(TURNED_BANKS):
@@ -198,30 +224,25 @@ def tile_improvedattention_pa_kernel(
                 )
             if t == 0:
                 quantise_tokens(1)
-            result = results.tile([P, 3 * HEADS, D], F32)
-            bias_heads = bias[:].rearrange("p (h d) -> p h d", d=D)
-            for n in range(BANKS):
-                heads = slice(BANK_HEADS * n, BANK_HEADS * (n + 1))
-                plain = slice(HALF, D) if n < TURNED_BANKS else slice(0, D)
-                nc.vector.tensor_tensor(
-                    out=result[:, heads, plain], in0=sums[n][:, :, plain], in1=bias_heads[:, heads, plain], op=ADD
+            for n in range(TURNED_BANKS if last else BANKS):
+                add_bias(n)
+            if not last:
+                store(2)
+            adder = nc.vector if last else nc.gpsimd
+            shares = [(0, HEADS), (HEADS, 2 * HEADS)] if t >= TOKEN_TILES - 2 else [(0, 2 * HEADS)]
+            for q0, q1 in shares:
+                turned = result[:, q0:q1, 0:HALF]
+                adder.tensor_tensor(
+                    out=turned.rearrange("p q (f i) -> p q f i", f=2),
+                    in0=products[:, q0:q1, 0, :].rearrange("p q (f i) -> p q f i", f=2),
+                    in1=products[:, q0:q1, 1, :].rearrange("p q (f i) -> p q f i", f=2)[:, :, ::-1, :],
+                    op=ADD,
                 )
-            adder = nc.vector if t == TOKEN_TILES - 1 else nc.gpsimd
-            turned = result[:, 0 : 2 * HEADS, 0:HALF]
-            adder.tensor_tensor(
-                out=turned.rearrange("p q (f i) -> p q f i", f=2),
-                in0=products[:, :, 0, :].rearrange("p q (f i) -> p q f i", f=2),
-                in1=products[:, :, 1, :].rearrange("p q (f i) -> p q f i", f=2)[:, :, ::-1, :],
-                op=ADD,
-            )
-            adder.tensor_tensor(
-                out=turned,
-                in0=turned,
-                in1=turned_bias[:, pt, :].rearrange("p (q j) -> p q j", j=HALF),
-                op=ADD,
-            )
-            for third in range(3):
-                nc.sync.dma_start(
-                    out=out_rows[third][P * t : P * (t + 1), :],
-                    in_=result[:, HEADS * third : HEADS * (third + 1), :].rearrange("p h d -> p (h d)"),
+                adder.tensor_tensor(
+                    out=turned,
+                    in0=turned,
+                    in1=turned_bias[:, pt, HALF * q0 : HALF * q1].rearrange("p (q j) -> p q j", j=HALF),
+                    op=ADD,
                 )
+                for third in range(q0 // HEADS, q1 // HEADS):
+                    store(third)

@@ -90,12 +90,12 @@ def tile_improvedattention_pa_kernel(
         nc.sync.dma_start(out=sin_raw[:], in_=sin_tab.rearrange("(t p) j -> p t j", p=P))
         load_x(0)
         load_w(0)
-        load_w(1)
         for r in range(4):
             nc.sync.dma_start(
                 out=w_planes[r:P:32, :, :].bitcast(I32),
                 in_=scale_words[:, r:16:4, :].rearrange("g c n -> c g n"),
             )
+        load_w(1)
         load_x(1)
         nc.sync.dma_start(out=bias[:], in_=b_qkv.partition_broadcast(P))
         load_w(2)

@@ -30,6 +30,9 @@ TURNED_BANKS = 2 * E // BANK
 POSITION_TILES = POSITIONS // P
 TOKEN_TILES = BATCH * POSITION_TILES
 
+SIDE_BLOCKS = E // P
+BANK_BLOCKS = BANK // P
+
 FLOPS = 2 * BATCH * POSITIONS * K * 3 * E
 
 
@@ -47,6 +50,7 @@ def tile_improvedattention_pa_kernel(
         partial = ctx.enter_context(tc.tile_pool(name="partial", bufs=3))
         psum_flip = ctx.enter_context(tc.psum_pool(name="psum_flip", bufs=2))
         psum_acc = ctx.enter_context(tc.psum_pool(name="psum_acc", bufs=BANKS))
+        sideways = ctx.enter_context(tc.tile_pool(name="sideways", bufs=1))
 
         warm = keep.tile([P, BANK], BF16)
         nc.vector.memset(warm[:], 0.0)
@@ -101,6 +105,9 @@ def tile_improvedattention_pa_kernel(
         load_w(2)
         for t in range(2, TOKEN_TILES):
             load_x(t)
+        side_rows = keep.tile([P, P], BF16)
+        nc.gpsimd.memset(side_rows[:], 0.0)
+        nc.sync.dma_start(out=side_rows[0:SIDE_BLOCKS, :], in_=b_qkv[2 * E : 3 * E].rearrange("(c p) -> c p", p=P))
 
         ident_f32 = keep.tile([P, P], F32)
         make_identity(nc, ident_f32[:])
@@ -173,10 +180,37 @@ def tile_improvedattention_pa_kernel(
                 quantise_tokens(t + 1)
             pt = t % POSITION_TILES
             last = t == TOKEN_TILES - 1
-            bank_order = list(range(BANKS))
-            if last:
-                bank_order = bank_order[TURNED_BANKS:] + bank_order[:TURNED_BANKS]
+            bank_order = list(range(TURNED_BANKS if last else BANKS))
             sums = {}
+            if last:
+                side_flipped = psum_flip.tile([P, P], BF16, tag="flip")
+                nc.tensor.transpose(side_flipped[:], side_rows[:], ident_bf16[:])
+                side_bias = keep.tile([P, SIDE_BLOCKS], F32)
+                nc.scalar.copy(out=side_bias[:], in_=side_flipped[:, 0:SIDE_BLOCKS])
+                side_out = sideways.tile([P, SIDE_BLOCKS, P], F32)
+                for half in range(SIDE_BLOCKS // BANK_BLOCKS):
+                    flat = psum_flip.tile([P, BANK_BLOCKS, P], F32, tag="flip")
+                    for i in range(BANK_BLOCKS):
+                        c = BANK_BLOCKS * half + i
+                        for g in range(PASSES):
+                            nc.tensor.matmul_mx(
+                                out=flat[:, i, :],
+                                lhsT=w_codes[2][:, g, 2 * P * c : 2 * P * (c + 1)].bitcast(FP4X4),
+                                lhsT_scale=w_planes[:, g, 2 * E + P * c : 2 * E + P * (c + 1)],
+                                rhs=x_codes[:, t, g, :].bitcast(FP8X4),
+                                rhs_scale=x_planes[:, t, g, :],
+                                start=(g == 0),
+                                stop=(g == PASSES - 1),
+                            )
+                    for i in range(BANK_BLOCKS):
+                        c = BANK_BLOCKS * half + i
+                        nc.scalar.activation(
+                            out=side_out[:, c, :],
+                            in_=flat[:, i, :],
+                            func=mybir.ActivationFunctionType.Identity,
+                            bias=side_bias[:, c : c + 1],
+                            scale=1.0,
+                        )
             for n in bank_order:
                 if n == TURNED_BANKS and t < POSITION_TILES:
                     turn_bias(pt)
@@ -210,8 +244,14 @@ def tile_improvedattention_pa_kernel(
                 )
 
             if last:
-                for n in range(TURNED_BANKS, BANKS):
-                    add_bias(n)
+                for half in range(SIDE_BLOCKS // BANK_BLOCKS):
+                    upright = psum_flip.tile([P, BANK_BLOCKS, P], F32, tag="flip")
+                    for i in range(BANK_BLOCKS):
+                        nc.tensor.transpose(upright[:, i, :], side_out[:, BANK_BLOCKS * half + i, :], ident_f32[:])
+                    heads = slice(2 * HEADS + BANK_HEADS * half, 2 * HEADS + BANK_HEADS * (half + 1))
+                    nc.scalar.copy(
+                        out=result[:, heads, :].rearrange("p h d -> p (h d)"), in_=upright[:].rearrange("p i f -> p (i f)")
+                    )
                 store(2)
             factors = table[:, pt, 0:D].rearrange("p (c j) -> p c j", c=2).unsqueeze(1)
             products = partial.tile([P, 2 * HEADS, 2, HALF], F32)

@@ -40,8 +40,8 @@ def tile_improvedattention_pa_kernel(
     tc, x, w_words, w_scales, b_qkv, sin_tab, cos_tab, out_q, out_k, out_v
 ):
     nc = tc.nc
-    x_rows = x.flatten_outer_dims()
-    out_rows = [o.rearrange("b s h d -> (b s) (h d)") for o in (out_q, out_k, out_v)]
+    x_tiles = x.rearrange("b (p i) k -> b i p k", i=POSITION_TILES)
+    out_tiles = [o.rearrange("b (p i) h d -> b i p (h d)", i=POSITION_TILES) for o in (out_q, out_k, out_v)]
 
     with ExitStack() as ctx:
         keep = ctx.enter_context(tc.tile_pool(name="keep", bufs=1))
@@ -73,11 +73,12 @@ def tile_improvedattention_pa_kernel(
             keep.tile([P, PASSES, 2 * E], U8, align_bytes=64, name="w_codes_%d" % third) for third in range(3)
         ]
         sin_raw = keep.tile([P, POSITION_TILES, HALF], BF16)
+        cos_raw = keep.tile([P, POSITION_TILES, HALF], BF16)
         table = keep.tile([P, POSITION_TILES, P], BF16)
         bias = keep.tile([P, 3 * E], BF16)
 
         def load_x(t):
-            nc.sync.dma_start(out=x_all[:, t, :], in_=x_rows[P * t : P * (t + 1), :])
+            nc.sync.dma_start(out=x_all[:, t, :], in_=x_tiles[t // POSITION_TILES, t % POSITION_TILES])
 
         def load_w(third):
             cols = slice(2 * E * third, 2 * E * (third + 1))
@@ -90,8 +91,8 @@ def tile_improvedattention_pa_kernel(
         nc.gpsimd.memset(b_rows[:], 0.0)
         b_turned = b_qkv[0 : 2 * E].rearrange("(k e d) -> k e d", e=2, d=D)[:, :, 0:HALF]
         nc.sync.dma_start(out=b_rows[0:HEADS, :, 0, :], in_=b_turned)
-        nc.sync.dma_start(out=table[:, :, 0:HALF], in_=cos_tab.rearrange("(t p) j -> p t j", p=P))
-        nc.sync.dma_start(out=sin_raw[:], in_=sin_tab.rearrange("(t p) j -> p t j", p=P))
+        nc.sync.dma_start(out=cos_raw[:], in_=cos_tab.rearrange("(p i) j -> p i j", i=POSITION_TILES))
+        nc.sync.dma_start(out=sin_raw[:], in_=sin_tab.rearrange("(p i) j -> p i j", i=POSITION_TILES))
         load_x(0)
         load_w(0)
         for r in range(4):
@@ -114,6 +115,7 @@ def tile_improvedattention_pa_kernel(
         ident_bf16 = keep.tile([P, P], BF16)
         make_identity(nc, ident_bf16[:])
 
+        nc.scalar.copy(out=table[:, :, 0:HALF], in_=cos_raw[:])
         nc.scalar.copy(out=table[:, :, HALF : HALF + QUARTER], in_=sin_raw[:, :, QUARTER:HALF])
         nc.scalar.mul(out=table[:, :, HALF + QUARTER : D], in_=sin_raw[:, :, 0:QUARTER], mul=-1.0)
         nc.scalar.copy(out=table[:, :, D:P], in_=table[:, :, 0:D])
@@ -239,7 +241,7 @@ def tile_improvedattention_pa_kernel(
 
             def store(third):
                 nc.sync.dma_start(
-                    out=out_rows[third][P * t : P * (t + 1), :],
+                    out=out_tiles[third][t // POSITION_TILES, t % POSITION_TILES],
                     in_=result[:, HEADS * third : HEADS * (third + 1), :].rearrange("p h d -> p (h d)"),
                 )
 

from contextlib import ExitStack

import concourse.mybir as mybir
from concourse.masks import make_identity

F32 = mybir.dt.float32
BF16 = mybir.dt.bfloat16
I32 = mybir.dt.int32
U8 = mybir.dt.uint8
U32 = mybir.dt.uint32
FP8X4 = mybir.dt.float8_e4m3fn_x4
FP4X4 = mybir.dt.float4_e2m1fn_x4
ADD = mybir.AluOpType.add
MULT = mybir.AluOpType.mult

P = 128
BATCH = 2
POSITIONS = 512
K = 1024
PASSES = K // (4 * P)
HEADS = 16
D = 64
HALF = D // 2
QUARTER = HALF // 2
E = HEADS * D
BANK = 512
BANK_HEADS = BANK // D
BANKS = 3 * E // BANK
TURNED_BANKS = 2 * E // BANK
POSITION_TILES = POSITIONS // P
TOKEN_TILES = BATCH * POSITION_TILES

SIDE_BLOCKS = E // P
BANK_BLOCKS = BANK // P

FLOPS = 2 * BATCH * POSITIONS * K * 3 * E


def tile_improvedattention_pa_kernel(
    tc, x, w_words, w_scales, b_qkv, sin_tab, cos_tab, out_q, out_k, out_v
):
    nc = tc.nc
    x_tiles = x.rearrange("b (p i) k -> b i p k", i=POSITION_TILES)
    out_tiles = [o.rearrange("b (p i) h d -> b i p (h d)", i=POSITION_TILES) for o in (out_q, out_k, out_v)]

    with ExitStack() as ctx:
        keep = ctx.enter_context(tc.tile_pool(name="keep", bufs=1))
        stage = ctx.enter_context(tc.tile_pool(name="stage", bufs=2))
        results = ctx.enter_context(tc.tile_pool(name="results", bufs=4))
        partial = ctx.enter_context(tc.tile_pool(name="partial", bufs=3))
        psum_flip = ctx.enter_context(tc.psum_pool(name="psum_flip", bufs=2))
        psum_acc = ctx.enter_context(tc.psum_pool(name="psum_acc", bufs=BANKS))
        sideways = ctx.enter_context(tc.tile_pool(name="sideways", bufs=1))

        warm = keep.tile([P, BANK], BF16)
        nc.vector.memset(warm[:], 0.0)

        def warm_up(count):
            for i in range(count):
                idle = psum_acc.tile([P, BANK], F32, tag="acc")
                nc.tensor.matmul(out=idle[:], lhsT=warm[:, 0:P], rhs=warm[:], start=True, stop=True)

        warm_up(4)
        first = keep.tile([P, 1], BF16)
        nc.scalar.copy(out=first[:], in_=warm[:, 0:1])

        w_planes = keep.tile([P, PASSES, 3 * E], U8, align_bytes=64)
        nc.vector.memset(w_planes[:].bitcast(I32), 0)
        scale_words = w_scales.bitcast(I32)

        x_all = keep.tile([P, TOKEN_TILES, K], BF16)
        w_codes = [
            keep.tile([P, PASSES, 2 * E], U8, align_bytes=64, name="w_codes_%d" % third) for third in range(3)
        ]
        sin_raw = keep.tile([P, POSITION_TILES, HALF], BF16)
        cos_raw = keep.tile([P, POSITION_TILES, HALF], BF16)
        table = keep.tile([P, POSITION_TILES, P], BF16)
        bias = keep.tile([P, 3 * E], BF16)

        def load_x(t):
            nc.sync.dma_start(out=x_all[:, t, :], in_=x_tiles[t // POSITION_TILES, t % POSITION_TILES])

        def load_w(third):
            cols = slice(2 * E * third, 2 * E * (third + 1))
            nc.sync.dma_start(
                out=w_codes[third][:].bitcast(I32),
                in_=w_words[:, :, cols].bitcast(I32).rearrange("g p c -> p g c"),
            )

        b_rows = keep.tile([P, 2, 2, HALF], BF16)
        nc.gpsimd.memset(b_rows[:], 0.0)
        b_turned = b_qkv[0 : 2 * E].rearrange("(k e d) -> k e d", e=2, d=D)[:, :, 0:HALF]
        nc.sync.dma_start(out=b_rows[0:HEADS, :, 0, :], in_=b_turned)
        nc.sync.dma_start(out=cos_raw[:], in_=cos_tab.rearrange("(p i) j -> p i j", i=POSITION_TILES))
        nc.sync.dma_start(out=sin_raw[:], in_=sin_tab.rearrange("(p i) j -> p i j", i=POSITION_TILES))
        load_x(0)
        load_w(0)
        for r in range(4):
            nc.sync.dma_start(
                out=w_planes[r:P:32, :, :].bitcast(I32),
                in_=scale_words[:, r:16:4, :].rearrange("g c n -> c g n"),
            )
        load_w(1)
        load_x(1)
        nc.sync.dma_start(out=bias[:], in_=b_qkv.partition_broadcast(P))
        load_w(2)
        for t in range(2, TOKEN_TILES):
            load_x(t)
        side_rows = keep.tile([P, P], BF16)
        nc.gpsimd.memset(side_rows[:], 0.0)
        nc.sync.dma_start(out=side_rows[0:SIDE_BLOCKS, :], in_=b_qkv[2 * E : 3 * E].rearrange("(c p) -> c p", p=P))

        ident_f32 = keep.tile([P, P], F32)
        make_identity(nc, ident_f32[:])
        ident_bf16 = keep.tile([P, P], BF16)
        make_identity(nc, ident_bf16[:])

        nc.scalar.copy(out=table[:, :, 0:HALF], in_=cos_raw[:])
        nc.scalar.copy(out=table[:, :, HALF : HALF + QUARTER], in_=sin_raw[:, :, QUARTER:HALF])
        nc.scalar.mul(out=table[:, :, HALF + QUARTER : D], in_=sin_raw[:, :, 0:QUARTER], mul=-1.0)
        nc.scalar.copy(out=table[:, :, D:P], in_=table[:, :, 0:D])

        x_codes = keep.tile([P, TOKEN_TILES, PASSES, P], U32, align_bytes=64)
        x_planes = keep.tile([P, TOKEN_TILES, PASSES, P], U8, align_bytes=64)

        def quantise_tokens(t):
            words = x_all[:, t, :].bitcast(F32)
            flipped = psum_flip.tile([P, PASSES, 2, P], F32, tag="flip")
            for g in range(PASSES):
                for u in range(2):
                    nc.tensor.transpose(
                        flipped[:, g, u, :], words[:, 256 * g + u : 256 * (g + 1) : 2], ident_f32[:]
                    )
            grouped = stage.tile([P, PASSES, P, 4], BF16, align_bytes=64)
            nc.scalar.copy(out=grouped[:].bitcast(F32), in_=flipped[:].rearrange("p g u r -> p g r u"))
            nc.vector.quantize_mx(
                out=x_codes[:, t].rearrange("p g r -> p (g r)").bitcast(FP8X4),
                scales=x_planes[:, t].rearrange("p g r -> p (g r)"),
                in_=grouped[:].rearrange("p g r j -> p (g r j)"),
            )

        quantise_tokens(0)
        warm_up(2)

        nc.scalar.copy(out=b_rows[:, :, 1, :], in_=b_rows[:, :, 0, :])
        b_flipped = psum_flip.tile([P, P], BF16, tag="flip")
        nc.tensor.transpose(b_flipped[:], b_rows[:].rearrange("p e c d -> p (e c d)"), ident_bf16[:])
        b_cols = keep.tile([P, HEADS], BF16)
        nc.scalar.copy(out=b_cols[:], in_=b_flipped[:, 0:HEADS])
        ident_parts = ident_bf16[:].rearrange("p (e c f i) -> p e c f i", e=2, c=2, f=2)
        place = keep.tile([P, 2, 2, QUARTER], BF16)
        nc.vector.tensor_tensor(out=place[:], in0=ident_parts[:, :, 0, :, :], in1=ident_parts[:, :, 1, ::-1, :], op=ADD)
        diagonals = keep.tile([P, HEADS, D], BF16)
        nc.vector.tensor_tensor(
            out=diagonals[:],
            in0=b_cols[:].unsqueeze(2).to_broadcast([P, HEADS, D]),
            in1=place[:].rearrange("p e f i -> p (e f i)").unsqueeze(1).to_broadcast([P, HEADS, D]),
            op=MULT,
        )
        table_flipped = psum_flip.tile([P, POSITION_TILES, P], BF16, tag="flip")
        for pt in range(POSITION_TILES):
            nc.tensor.transpose(table_flipped[:, pt, :], table[:, pt, :], ident_bf16[:])
        table_t = keep.tile([P, POSITION_TILES, P], BF16)
        nc.scalar.copy(out=table_t[:], in_=table_flipped[:])
        turned_bias = keep.tile([P, POSITION_TILES, 2 * HEADS * HALF], F32)

        def turn_bias(pt):
            for half in range(2 * HEADS * HALF // BANK):
                cols = slice(BANK * half, BANK * (half + 1))
                made = psum_flip.tile([P, BANK], F32, tag="flip")
                nc.tensor.matmul(
                    out=made[:],
                    lhsT=table_t[:, pt, :],
                    rhs=diagonals[:].rearrange("p q j -> p (q j)")[:, cols],
                    start=True,
                    stop=True,
                )
                nc.scalar.copy(out=turned_bias[:, pt, cols], in_=made[:])

        for t in range(TOKEN_TILES):
            if 0 < t < TOKEN_TILES - 1:
                quantise_tokens(t + 1)
            pt = t % POSITION_TILES
            last = t == TOKEN_TILES - 1
            bank_order = list(range(TURNED_BANKS if last else BANKS))
            sums = {}
            if last:
                side_flipped = psum_flip.tile([P, P], BF16, tag="flip")
                nc.tensor.transpose(side_flipped[:], side_rows[:], ident_bf16[:])
                side_bias = keep.tile([P, SIDE_BLOCKS], F32)
                nc.scalar.copy(out=side_bias[:], in_=side_flipped[:, 0:SIDE_BLOCKS])
                side_out = sideways.tile([P, SIDE_BLOCKS, P], F32)
                for half in range(SIDE_BLOCKS // BANK_BLOCKS):
                    flat = psum_flip.tile([P, BANK_BLOCKS, P], F32, tag="flip")
                    for i in range(BANK_BLOCKS):
                        c = BANK_BLOCKS * half + i
                        for g in range(PASSES):
                            nc.tensor.matmul_mx(
                                out=flat[:, i, :],
                                lhsT=w_codes[2][:, g, 2 * P * c : 2 * P * (c + 1)].bitcast(FP4X4),
                                lhsT_scale=w_planes[:, g, 2 * E + P * c : 2 * E + P * (c + 1)],
                                rhs=x_codes[:, t, g, :].bitcast(FP8X4),
                                rhs_scale=x_planes[:, t, g, :],
                                start=(g == 0),
                                stop=(g == PASSES - 1),
                            )
                    for i in range(BANK_BLOCKS):
                        c = BANK_BLOCKS * half + i
                        nc.scalar.activation(
                            out=side_out[:, c, :],
                            in_=flat[:, i, :],
                            func=mybir.ActivationFunctionType.Identity,
                            bias=side_bias[:, c : c + 1],
                            scale=1.0,
                        )
            for n in bank_order:
                if n == TURNED_BANKS and t < POSITION_TILES:
                    turn_bias(pt)
                acc = psum_acc.tile([P, BANK], F32, tag="acc")
                for g in range(PASSES):
                    nc.tensor.matmul_mx(
                        out=acc[:],
                        lhsT=x_codes[:, t, g, :].bitcast(FP8X4),
                        lhsT_scale=x_planes[:, t, g, :],
                        rhs=w_codes[n // 2][:, g, 2 * BANK * (n % 2) : 2 * BANK * (n % 2 + 1)].bitcast(FP4X4),
                        rhs_scale=w_planes[:, g, BANK * n : BANK * (n + 1)],
                        start=(g == 0),
                        stop=(g == PASSES - 1),
                    )
                sums[n] = acc[:].rearrange("p (h d) -> p h d", d=D)

            result = results.tile([P, 3 * HEADS, D], F32)
            bias_heads = bias[:].rearrange("p (h d) -> p h d", d=D)

            def add_bias(n):
                heads = slice(BANK_HEADS * n, BANK_HEADS * (n + 1))
                plain = slice(HALF, D) if n < TURNED_BANKS else slice(0, D)
                nc.vector.tensor_tensor(
                    out=result[:, heads, plain], in0=sums[n][:, :, plain], in1=bias_heads[:, heads, plain], op=ADD
                )

            def store(third):
                nc.sync.dma_start(
                    out=out_tiles[third][t // POSITION_TILES, t % POSITION_TILES],
                    in_=result[:, HEADS * third : HEADS * (third + 1), :].rearrange("p h d -> p (h d)"),
                )

            if last:
                for half in range(SIDE_BLOCKS // BANK_BLOCKS):
                    upright = psum_flip.tile([P, BANK_BLOCKS, P], F32, tag="flip")
                    for i in range(BANK_BLOCKS):
                        nc.tensor.transpose(upright[:, i, :], side_out[:, BANK_BLOCKS * half + i, :], ident_f32[:])
                    heads = slice(2 * HEADS + BANK_HEADS * half, 2 * HEADS + BANK_HEADS * (half + 1))
                    nc.scalar.copy(
                        out=result[:, heads, :].rearrange("p h d -> p (h d)"), in_=upright[:].rearrange("p i f -> p (i f)")
                    )
                store(2)
            factors = table[:, pt, 0:D].rearrange("p (c j) -> p c j", c=2).unsqueeze(1)
            products = partial.tile([P, 2 * HEADS, 2, HALF], F32)
            for n in range(TURNED_BANKS):
                nc.vector.tensor_tensor(
                    out=products[:, BANK_HEADS * n : BANK_HEADS * (n + 1), :, :],
                    in0=sums[n][:, :, 0:HALF].unsqueeze(2).to_broadcast([P, BANK_HEADS, 2, HALF]),
                    in1=factors.to_broadcast([P, BANK_HEADS, 2, HALF]),
                    op=MULT,
                )
            if t == 0:
                quantise_tokens(1)
            for n in range(TURNED_BANKS if last else BANKS):
                add_bias(n)
            if not last:
                store(2)
            adder = nc.vector if last else nc.gpsimd
            shares = [(0, HEADS), (HEADS, 2 * HEADS)] if t >= TOKEN_TILES - 2 else [(0, 2 * HEADS)]
            for q0, q1 in shares:
                turned = result[:, q0:q1, 0:HALF]
                adder.tensor_tensor(
                    out=turned.rearrange("p q (f i) -> p q f i", f=2),
                    in0=products[:, q0:q1, 0, :].rearrange("p q (f i) -> p q f i", f=2),
                    in1=products[:, q0:q1, 1, :].rearrange("p q (f i) -> p q f i", f=2)[:, :, ::-1, :],
                    op=ADD,
                )
                adder.tensor_tensor(
                    out=turned,
                    in0=turned,
                    in1=turned_bias[:, pt, HALF * q0 : HALF * q1].rearrange("p (q j) -> p q j", j=HALF),
                    op=ADD,
                )
                for third in range(q0 // HEADS, q1 // HEADS):
                    store(third)
